import numpy as np
import ml_dtypes


def mxq(x, axis, fmt="e4m3"):
    dtype, down = {"e4m3": (ml_dtypes.float8_e4m3fn, 7), "e5m2": (ml_dtypes.float8_e5m2, 14)}[fmt]
    v = np.moveaxis(np.asarray(x, np.float32).astype(ml_dtypes.bfloat16).astype(np.float64), axis, -1)
    blocks = v.reshape(v.shape[:-1] + (-1, 32))
    amax = np.abs(blocks).max(-1, keepdims=True)
    byte = np.maximum(np.where(amax > 0, np.frexp(amax)[1] - 1 + 127, 0) - down, 1)
    scale = np.exp2(byte - 127.0)
    codes = (blocks / scale).astype(np.float32).astype(dtype).astype(np.float64)
    return np.moveaxis((codes * scale).reshape(v.shape), -1, axis)


WIDE = False


def mx_kscale(k):
    if not WIDE:
        return np.ones(k)
    levels = np.array([10, -10, 5, -5, 0])
    if k % 512:
        return np.exp2(np.random.permutation(np.resize(levels, k // 32))).repeat(32)
    a = np.empty((k // 512, 16))
    for p in range(k // 512):
        a[p, :8] = np.random.permutation(np.resize(levels, 8))
        for g in range(8):
            far = levels[np.abs(levels - a[p, g]) >= 10]
            a[p, g + 8] = far[np.random.randint(len(far))]
    return np.exp2(a.ravel()).repeat(32)


BF16 = ml_dtypes.bfloat16


def bf(x):
    return np.asarray(x, np.float32).astype(BF16)


def f64(x):
    return np.asarray(x).astype(np.float64)


B, D_IN, D_H = 512, 1024, 1024


def setup_inputs():
    s, t = mx_kscale(D_IN), mx_kscale(D_H)
    inp = {"x": bf(np.random.standard_normal((B, D_IN)) * s),
           "h_prev": bf(np.random.standard_normal((B, D_H)) * t),
           "c_prev": bf(np.random.standard_normal((B, D_H))),
           "n_prev": bf(np.random.uniform(size=(B, D_H)))}
    for g in ("i", "f", "z"):
        inp["W_" + g] = bf(np.random.standard_normal((D_IN, D_H)) * 0.5 / np.sqrt(D_IN) / s[:, None])
        inp["b_" + g] = bf(np.random.standard_normal(D_H) * 0.3)
        inp["U_" + g] = bf(np.random.standard_normal((D_H, D_H)) * 0.5 / np.sqrt(D_H) / t[:, None])
    return inp


def reference(x, h_prev, c_prev, n_prev, W_i, b_i, U_i, W_f, b_f, U_f, W_z, b_z, U_z):
    xq = mxq(f64(x), 1, "e4m3")
    hq = mxq(f64(h_prev), 1, "e4m3")
    i = np.exp((xq @ mxq(f64(W_i), 0, "e4m3")) + f64(b_i) + (hq @ mxq(f64(U_i), 0, "e4m3")))
    f = np.exp((xq @ mxq(f64(W_f), 0, "e4m3")) + f64(b_f) + (hq @ mxq(f64(U_f), 0, "e4m3")))
    z = np.tanh((xq @ mxq(f64(W_z), 0, "e4m3")) + f64(b_z) + (hq @ mxq(f64(U_z), 0, "e4m3")))
    c = f * f64(c_prev) + i * z
    n = f * f64(n_prev) + i
    return (c, n)

@@ -1,0 +1,385 @@
+from contextlib import ExitStack
+
+import concourse.mybir as mybir
+from concourse.masks import make_identity
+
+FLOPS = 6 * 2 * 512 * 1024 * 1024
+
+BF16 = mybir.dt.bfloat16
+F32 = mybir.dt.float32
+U32 = mybir.dt.uint32
+U8 = mybir.dt.uint8
+FP8X4 = mybir.dt.float8_e4m3fn_x4
+ACT = mybir.ActivationFunctionType
+ALU = mybir.AluOpType
+
+P = 128
+RAW_SLOTS = 6
+PINNED = False
+V_COLS_F = 288
+V_COLS_I = 192
+Z_V_CHUNKS = (1, 2, 1, 2, 1, 2, 1, 2)
+STORES = ((0, 1), (2, 3), (4, 5), (6,), (7,))
+F_BUFS = 8
+LOOK = 2
+GF, GI, GZ = 0, 1, 2
+
+
+def tile_slstmcell_pa_kernel(
+    tc, x, h_prev, c_prev, n_prev, W_i, b_i, U_i, W_f, b_f, U_f, W_z, b_z, U_z, out_0, out_1
+):
+    nc = tc.nc
+    with ExitStack() as ctx:
+        if PINNED:
+            ctx.enter_context(tc.manual_schedule())
+        const = ctx.enter_context(tc.tile_pool(name="const", bufs=1))
+        keep = ctx.enter_context(tc.tile_pool(name="keep", bufs=1))
+        rawp = ctx.enter_context(tc.tile_pool(name="rawp", bufs=RAW_SLOTS))
+        grpp = ctx.enter_context(tc.tile_pool(name="grpp", bufs=4))
+        gxp = ctx.enter_context(tc.tile_pool(name="gxp", bufs=2))
+        gatep = ctx.enter_context(tc.tile_pool(name="gatep", bufs=2))
+        accp = ctx.enter_context(tc.psum_pool(name="psum", bufs=8))
+        trp = accp
+        flexp = accp
+        fpool = ctx.enter_context(tc.tile_pool(name="fpool", bufs=F_BUFS))
+
+        weights = ((W_f, U_f), (W_i, U_i), (W_z, U_z))
+        biases = (b_f, b_i, b_z)
+
+        bias_rows = const.tile([P, P], BF16)
+        nc.vector.memset(bias_rows[:], 0.0)
+        ident32 = const.tile([P, P], F32)
+        make_identity(nc, ident32[:])
+        ident16 = const.tile([P, P], BF16)
+        make_identity(nc, ident16[:])
+        bias_sb = const.tile([P, 24], F32)
+
+        codes = [keep.tile([P, 1024], U32, name="codes%d" % c, align_bytes=64) for c in range(12)]
+        planes = [keep.tile([P, 1024], U8, name="planes%d" % c, align_bytes=64) for c in range(12)]
+        xcodes = [keep.tile([P, 512], U32, name="xcodes%d" % c, align_bytes=64) for c in range(4)]
+        xplanes = [keep.tile([P, 512], U8, name="xplanes%d" % c, align_bytes=64) for c in range(4)]
+        cn_sb = keep.tile([P, 2, 4, 1024], BF16)
+        i_sb = [keep.tile([P, 512], F32, name="i_sb%d" % m) for m in range(8)]
+        cn_out = [keep.tile([P, 2, 4, P * len(grp)], F32, name="cn_out%d" % grp[0]) for grp in STORES]
+
+        out_c = out_0.rearrange("(p a) h -> p a h", a=4)
+        out_n = out_1.rearrange("(p a) h -> p a h", a=4)
+
+        load_order = [("w", 0, 0), ("a", 0, 0), ("w", 0, 1), ("a", 1, 0), ("w", 0, 2), ("w", 0, 3)]
+        load_order += [("w", 1, 0), ("c", 0, 0), ("c", 1, 0), ("w", 1, 1), ("w", 1, 2), ("w", 1, 3)]
+        load_order += [("w", 2, c) for c in range(4)]
+        raw_tiles = {}
+        state = {"load": 0}
+
+        def issue_next_load():
+            k = state["load"]
+            if k >= len(load_order):
+                return
+            state["load"] = k + 1
+            kind, g, c = load_order[k]
+            if kind == "c":
+                src = (c_prev, n_prev)[g]
+                nc.sync.dma_start(out=cn_sb[:, g], in_=src.rearrange("(p a) h -> p a h", a=4))
+                issue_next_load()
+                return
+            if k == 0:
+                halves = rawp.tile([P, 2, 4, 512], BF16, tag="raw")
+                raw_tiles["first"] = halves
+                for b in range(2):
+                    for u in range(2):
+                        nc.sync.dma_start(
+                            out=halves[:, b, 2 * u : 2 * u + 2, :],
+                            in_=weights[0][0][0:512, 512 * b : 512 * b + 512].rearrange(
+                                "(p e) n -> p e n", e=4
+                            )[:, 2 * u : 2 * u + 2, :],
+                        )
+                return
+            raw = rawp.tile([P, 4, 1024], BF16, tag="raw", name="raw%d" % k)
+            raw_tiles[load_order[k]] = raw
+            if kind == "w":
+                w = weights[g][c // 2]
+                r0 = 512 * (c % 2)
+                nc.sync.dma_start(
+                    out=raw[:],
+                    in_=w[r0 : r0 + 512, :].rearrange("(p e) n -> p e n", e=4),
+                )
+            else:
+                src = x if g == 0 else h_prev
+                nc.sync.dma_start(out=raw[:], in_=src.rearrange("(p a) k -> p a k", a=4))
+
+        for k in range(RAW_SLOTS):
+            issue_next_load()
+            if k == 1:
+                for g in range(3):
+                    nc.sync.dma_start(
+                        out=bias_rows[8 * g : 8 * g + 8, :],
+                        in_=biases[g].rearrange("(m c) -> m c", c=P),
+                    )
+
+        def regroup(eng, dst, src):
+            o = dst.rearrange("p (c i) t -> p c t i", i=4)
+            s = src.rearrange("p t (c i) -> p c t i", i=4)
+            if eng == "v":
+                nc.vector.tensor_copy(out=o, in_=s)
+            else:
+                nc.scalar.copy(out=o, in_=s)
+
+        grps = {}
+
+        def rg_unit(g, u, vcols):
+            c, c0 = u // 2, 512 * (u % 2)
+            if g == 0 and c == 0:
+                src = raw_tiles["first"][:, u]
+            else:
+                src = raw_tiles[("w", g, c)][:, :, c0 : c0 + 512]
+            grp = grpp.tile([P, 512, 4], BF16, tag="grp", name="grp_%d_%d" % (g, u), align_bytes=64)
+            grps[(g, u)] = grp
+            regroup("v", grp[:, 0:vcols, :], src[:, :, 0:vcols])
+            regroup("s", grp[:, vcols:512, :], src[:, :, vcols:512])
+
+        def q_unit(g, u):
+            c, c0 = u // 2, 512 * (u % 2)
+            nc.vector.quantize_mx(
+                out=codes[4 * g + c][:, c0 : c0 + 512].bitcast(FP8X4),
+                scales=planes[4 * g + c][:, c0 : c0 + 512],
+                in_=grps[(g, u)][:].rearrange("p w t -> p (w t)"),
+            )
+
+        def rg_ztile(m, v_chunks):
+            grp = grpp.tile([P, 512, 4], BF16, tag="grp", name="grp_z_%d" % m, align_bytes=64)
+            grps[(GZ, m)] = grp
+            for c in range(4):
+                raw = raw_tiles[("w", GZ, c)]
+                regroup(
+                    "v" if c >= 4 - v_chunks else "s",
+                    grp[:, P * c : P * c + P, :],
+                    raw[:, :, P * m : P * m + P],
+                )
+
+        def q_ztile(m):
+            c0 = 512 * (m % 2)
+            nc.vector.quantize_mx(
+                out=codes[8 + m // 2][:, c0 : c0 + 512].bitcast(FP8X4),
+                scales=planes[8 + m // 2][:, c0 : c0 + 512],
+                in_=grps[(GZ, m)][:].rearrange("p w t -> p (w t)"),
+            )
+
+        def stationary(g, m, c):
+            if g == GZ:
+                t, c0 = 8 + m // 2, 512 * (m % 2) + P * c
+            else:
+                t, c0 = 4 * g + c, P * m
+            return codes[t][:, c0 : c0 + P].bitcast(FP8X4), planes[t][:, c0 : c0 + P]
+
+        gxs = {}
+        banks = {}
+
+        def xt(s, g, half):
+            words = raw_tiles[("a", s, 0)][:].bitcast(F32)
+            bank = (trp, flexp)[half].tile([P, 2, 2, P], F32, tag="bank", name="xt_%d_%d_%d" % (s, g, half))
+            banks[(s, g, half)] = bank
+            for a in range(2):
+                for u in range(2):
+                    w0 = 256 * g + u
+                    nc.tensor.transpose(
+                        bank[:, a, u, :], words[:, 2 * half + a, w0 : 256 * g + 256 : 2], ident32[:]
+                    )
+
+        def xc(s, g, half):
+            if half == 0:
+                gxs[(s, g)] = gxp.tile([P, 512, 4], BF16, tag="gx", name="gx_%d_%d" % (s, g), align_bytes=64)
+            gx32 = gxs[(s, g)][:].bitcast(F32)
+            nc.scalar.copy(
+                out=gx32[:, 256 * half : 256 * half + 256, :].rearrange("p (a b) u -> p a b u", a=2),
+                in_=banks[(s, g, half)][:].rearrange("p a u b -> p a b u"),
+            )
+
+        def xq(s, g):
+            nc.vector.quantize_mx(
+                out=xcodes[2 * s + g][:].bitcast(FP8X4),
+                scales=xplanes[2 * s + g][:],
+                in_=gxs[(s, g)][:].rearrange("p w t -> p (w t)"),
+            )
+
+        accs = {}
+
+        def mx_pass(g, m, c, pool=None):
+            if c == 0:
+                pl = pool or accp
+                accs[(g, m)] = pl.tile([P, 512], F32, tag="bank", name="acc_%d_%d" % (g, m))
+            lhsT, lhsT_scale = stationary(g, m, c)
+            nc.tensor.matmul_mx(
+                out=accs[(g, m)][:],
+                lhsT=lhsT,
+                lhsT_scale=lhsT_scale,
+                rhs=xcodes[c][:].bitcast(FP8X4),
+                rhs_scale=xplanes[c][:],
+                start=(c == 0),
+                stop=(c == 3),
+            )
+
+        def mx(g, m, pool=None):
+            for c in range(4):
+                mx_pass(g, m, c, pool)
+
+        sb = {}
+
+        def gate_act(g, m):
+            if g == GI:
+                dst = i_sb[m]
+            else:
+                dst = (fpool if g == GF else gatep).tile([P, 512], F32, tag="g%d" % g, name="gate_%d_%d" % (g, m))
+            sb[(g, m)] = dst
+            nc.scalar.activation(
+                out=dst[:],
+                in_=accs[(g, m)][:],
+                func=(ACT.Tanh if g == GZ else ACT.Exp),
+                bias=bias_sb[:, 8 * g + m : 8 * g + m + 1],
+                scale=1.0,
+            )
+
+        flipped = {}
+
+        def flip(key, pool=None):
+            bank = (pool or trp).tile([P, 4, P], F32, tag="bank", name="T_%s_%d" % key)
+            flipped[key] = bank
+            src = sb[key]
+            for a in range(4):
+                nc.tensor.transpose(bank[:, a, :], src[:, P * a : P * a + P], ident32[:])
+
+        def part(m):
+            for j, grp in enumerate(STORES):
+                if m in grp:
+                    off = P * grp.index(m)
+                    return cn_out[j][:, :, :, off : off + P]
+
+        def store_if_full(which, m):
+            for j, grp in enumerate(STORES):
+                if m == grp[-1]:
+                    dram = (out_c, out_n)[which]
+                    nc.sync.dma_start(out=dram[:, :, P * grp[0] : P * grp[-1] + P], in_=cn_out[j][:, which])
+
+        def v_fc_fn(m):
+            fT = flipped[(GF, m)]
+            nc.vector.tensor_tensor(
+                out=part(m),
+                in0=fT[:].unsqueeze(1).to_broadcast([P, 2, 4, P]),
+                in1=cn_sb[:, :, :, P * m : P * m + P],
+                op=ALU.mult,
+            )
+
+        def v_n(m):
+            nc.vector.tensor_tensor(
+                out=part(m)[:, 1], in0=flipped[(GI, m)][:], in1=part(m)[:, 1], op=ALU.add
+            )
+            store_if_full(1, m)
+
+        def v_iz(m):
+            iz = gatep.tile([P, 512], F32, tag="iz", name="iz%d" % m)
+            sb[("iz", m)] = iz
+            nc.vector.tensor_tensor(out=iz[:], in0=i_sb[m][:], in1=sb[(GZ, m)][:], op=ALU.mult)
+
+        def v_c(m):
+            nc.vector.tensor_tensor(
+                out=part(m)[:, 0], in0=flipped[("iz", m)][:], in1=part(m)[:, 0], op=ALU.add
+            )
+            store_if_full(0, m)
+
+        def passes(g, c, tiles):
+            for m in tiles:
+                mx_pass(g, m, c)
+
+        LO, HI = (0, 1, 2, 3), (4, 5, 6, 7)
+        rg_unit(GF, 0, V_COLS_F)
+        rg_unit(GF, 1, V_COLS_F)
+        issue_next_load()
+        q_unit(GF, 0)
+        for g in range(2):
+            for half in range(2):
+                xt(0, g, half)
+                xc(0, g, half)
+        issue_next_load()
+        q_unit(GF, 1)
+        xq(0, 0)
+        rg_unit(GF, 2, V_COLS_F)
+        xq(0, 1)
+        passes(GF, 0, LO)
+        rg_unit(GF, 3, V_COLS_F)
+        issue_next_load()
+        q_unit(GF, 2)
+        for g in range(2):
+            for half in range(2):
+                xt(1, g, half)
+                xc(1, g, half)
+        issue_next_load()
+        passes(GF, 1, LO)
+        q_unit(GF, 3)
+        xq(1, 0)
+        rg_unit(GF, 4, V_COLS_F)
+        xq(1, 1)
+        bias_ps = trp.tile([P, P], BF16, tag="bank")
+        nc.tensor.transpose(bias_ps[:], bias_rows[:], ident16[:])
+        nc.vector.tensor_copy(out=bias_sb[:], in_=bias_ps[:, 0:24])
+        passes(GF, 0, HI)
+        passes(GF, 1, HI)
+        rg_unit(GF, 5, V_COLS_F)
+        issue_next_load()
+        q_unit(GF, 4)
+        passes(GF, 2, LO)
+        rg_unit(GF, 6, V_COLS_F)
+        q_unit(GF, 5)
+        passes(GF, 2, HI)
+        rg_unit(GF, 7, V_COLS_F)
+        issue_next_load()
+        q_unit(GF, 6)
+        passes(GF, 3, LO)
+
+        EARLY, LATE = (0, 1, 2, 3, 4, 5), (6, 7)
+        for s in range(8):
+            rg_unit(GI, s, V_COLS_I)
+            if s % 2 == 1:
+                issue_next_load()
+            if s == 0:
+                q_unit(GF, 7)
+                passes(GF, 3, HI)
+            else:
+                q_unit(GI, s - 1)
+                passes(GI, (s - 1) // 2, [m for m in (LO, HI)[(s - 1) % 2] if m in EARLY])
+            if s < 4:
+                for m in (2 * s, 2 * s + 1):
+                    gate_act(GF, m)
+                    flip((GF, m))
+            if 0 < s < 5:
+                v_fc_fn(2 * s - 2)
+                v_fc_fn(2 * s - 1)
+            if s == 5:
+                passes(GI, 0, LATE)
+                passes(GI, 1, LATE)
+            if s == 6:
+                passes(GI, 2, LATE)
+
+        for m in range(LOOK + 1):
+            rg_ztile(m, Z_V_CHUNKS[m])
+            if m == 0:
+                q_unit(GI, 7)
+                passes(GI, 3, HI)
+        for m in range(LOOK):
+            q_ztile(m)
+            mx(GZ, m)
+        gate_act(GI, 0)
+        flip((GI, 0))
+        for s in range(8):
+            if s + LOOK < 8:
+                q_ztile(s + LOOK)
+                mx(GZ, s + LOOK)
+            if s + LOOK + 1 < 8:
+                rg_ztile(s + LOOK + 1, Z_V_CHUNKS[s + LOOK + 1])
+            gate_act(GZ, s)
+            if s < 7:
+                gate_act(GI, s + 1)
+            v_iz(s)
+            flip(("iz", s))
+            if s < 7:
+                flip((GI, s + 1))
+            v_n(s)
+            v_c(s)

@@ -23,6 +23,7 @@ STORES = ((0, 1), (2, 3), (4, 5), (6,), (7,))
 F_BUFS = 8
 LOOK = 2
 GF, GI, GZ = 0, 1, 2
+WARM_UP = 14
 
 
 def tile_slstmcell_pa_kernel(
@@ -53,6 +54,9 @@ def tile_slstmcell_pa_kernel(
         ident16 = const.tile([P, P], BF16)
         make_identity(nc, ident16[:])
         bias_sb = const.tile([P, 24], F32)
+        zeros = const.tile([P, 512], BF16)
+        nc.vector.memset(zeros[:], 0.0)
+        warm_act = const.tile([P, 1], F32)
 
         codes = [keep.tile([P, 1024], U32, name="codes%d" % c, align_bytes=64) for c in range(12)]
         planes = [keep.tile([P, 1024], U8, name="planes%d" % c, align_bytes=64) for c in range(12)]
@@ -290,14 +294,19 @@ def tile_slstmcell_pa_kernel(
                 mx_pass(g, m, c)
 
         LO, HI = (0, 1, 2, 3), (4, 5, 6, 7)
-        rg_unit(GF, 0, V_COLS_F)
-        rg_unit(GF, 1, V_COLS_F)
-        issue_next_load()
-        q_unit(GF, 0)
-        for g in range(2):
-            for half in range(2):
-                xt(0, g, half)
-                xc(0, g, half)
+        with tc.manual_schedule(engines={mybir.EngineType.PE, mybir.EngineType.Activation}):
+            nc.scalar.activation(out=warm_act[:], in_=zeros[:, 0:1], func=ACT.Exp)
+            warm_bank = accp.tile([P, 512], F32, tag="bank")
+            for j in range(WARM_UP):
+                nc.tensor.matmul(warm_bank[:], lhsT=zeros[:, 0:P], rhs=zeros[:], start=True, stop=True)
+            rg_unit(GF, 0, V_COLS_F)
+            rg_unit(GF, 1, V_COLS_F)
+            issue_next_load()
+            q_unit(GF, 0)
+            for g in range(2):
+                for half in range(2):
+                    xt(0, g, half)
+                    xc(0, g, half)
         issue_next_load()
         q_unit(GF, 1)
         xq(0, 0)

@@ -18,7 +18,8 @@ RAW_SLOTS = 6
 PINNED = False
 V_COLS_F = 288
 V_COLS_I = 192
-Z_V_CHUNKS = (1, 2, 1, 2, 1, 2, 1, 2)
+Z_V_CHUNKS = (2, 2, 2, 2, 2, 2, 2, 2)
+GPSIMD_IZ = (0, 1, 2, 3, 4, 5, 6)
 STORES = ((0, 1), (2, 3), (4, 5), (6,), (7,))
 F_BUFS = 8
 LOOK = 2
@@ -281,7 +282,8 @@ def tile_slstmcell_pa_kernel(
         def v_iz(m):
             iz = gatep.tile([P, 512], F32, tag="iz", name="iz%d" % m)
             sb[("iz", m)] = iz
-            nc.vector.tensor_tensor(out=iz[:], in0=i_sb[m][:], in1=sb[(GZ, m)][:], op=ALU.mult)
+            eng = nc.gpsimd if m in GPSIMD_IZ else nc.vector
+            eng.tensor_tensor(out=iz[:], in0=i_sb[m][:], in1=sb[(GZ, m)][:], op=ALU.mult)
 
         def v_c(m):
             nc.vector.tensor_tensor(

@@ -17,14 +17,18 @@ P = 128
 RAW_SLOTS = 6
 PINNED = False
 V_COLS_F = 288
-V_COLS_I = 192
-Z_V_CHUNKS = (2, 2, 2, 2, 2, 2, 2, 2)
+V_COLS_I = (384, 384, 160, 160, 160, 160, 160, 160)
+Z_V_CHUNKS = (2, 1, 2, 1, 2, 1, 2, 1)
 GPSIMD_IZ = (0, 1, 2, 3, 4, 5, 6)
 STORES = ((0, 1), (2, 3), (4, 5), (6,), (7,))
 F_BUFS = 8
+GRP_BUFS = 7
+FIRST_LOADS = 6
 LOOK = 2
+F_ACTS = {0: (0, 1), 1: (2, 3, 4, 5, 6, 7)}
+F_PRODUCTS = {1: (0, 1), 2: (2, 3), 3: (4, 5), 4: (6, 7)}
 GF, GI, GZ = 0, 1, 2
-WARM_UP = 14
+WARM_UP = 10
 
 
 def tile_slstmcell_pa_kernel(
@@ -37,8 +41,8 @@ def tile_slstmcell_pa_kernel(
         const = ctx.enter_context(tc.tile_pool(name="const", bufs=1))
         keep = ctx.enter_context(tc.tile_pool(name="keep", bufs=1))
         rawp = ctx.enter_context(tc.tile_pool(name="rawp", bufs=RAW_SLOTS))
-        grpp = ctx.enter_context(tc.tile_pool(name="grpp", bufs=4))
-        gxp = ctx.enter_context(tc.tile_pool(name="gxp", bufs=2))
+        halfp = ctx.enter_context(tc.tile_pool(name="halfp", bufs=4))
+        grpp = ctx.enter_context(tc.tile_pool(name="grpp", bufs=GRP_BUFS))
         gatep = ctx.enter_context(tc.tile_pool(name="gatep", bufs=2))
         accp = ctx.enter_context(tc.psum_pool(name="psum", bufs=8))
         trp = accp
@@ -64,7 +68,6 @@ def tile_slstmcell_pa_kernel(
         xcodes = [keep.tile([P, 512], U32, name="xcodes%d" % c, align_bytes=64) for c in range(4)]
         xplanes = [keep.tile([P, 512], U8, name="xplanes%d" % c, align_bytes=64) for c in range(4)]
         cn_sb = keep.tile([P, 2, 4, 1024], BF16)
-        i_sb = [keep.tile([P, 512], F32, name="i_sb%d" % m) for m in range(8)]
         cn_out = [keep.tile([P, 2, 4, P * len(grp)], F32, name="cn_out%d" % grp[0]) for grp in STORES]
 
         out_c = out_0.rearrange("(p a) h -> p a h", a=4)
@@ -99,9 +102,9 @@ def tile_slstmcell_pa_kernel(
                             )[:, 2 * u : 2 * u + 2, :],
                         )
                 return
-            raw = rawp.tile([P, 4, 1024], BF16, tag="raw", name="raw%d" % k)
-            raw_tiles[load_order[k]] = raw
             if kind == "w":
+                raw = rawp.tile([P, 4, 1024], BF16, tag="raw", name="raw%d" % k)
+                raw_tiles[load_order[k]] = raw
                 w = weights[g][c // 2]
                 r0 = 512 * (c % 2)
                 nc.sync.dma_start(
@@ -110,9 +113,15 @@ def tile_slstmcell_pa_kernel(
                 )
             else:
                 src = x if g == 0 else h_prev
-                nc.sync.dma_start(out=raw[:], in_=src.rearrange("(p a) k -> p a k", a=4))
+                for half in range(2):
+                    k0 = 512 * half
+                    piece = halfp.tile([P, 4, 512], BF16, tag="half", name="half_%d_%d" % (g, half))
+                    raw_tiles[("half", g, half)] = piece
+                    nc.sync.dma_start(
+                        out=piece[:], in_=src[:, k0 : k0 + 512].rearrange("(p a) k -> p a k", a=4)
+                    )
 
-        for k in range(RAW_SLOTS):
+        for k in range(FIRST_LOADS):
             issue_next_load()
             if k == 1:
                 for g in range(3):
@@ -180,19 +189,16 @@ def tile_slstmcell_pa_kernel(
         banks = {}
 
         def xt(s, g, half):
-            words = raw_tiles[("a", s, 0)][:].bitcast(F32)
+            words = raw_tiles[("half", s, g)][:].bitcast(F32)
             bank = (trp, flexp)[half].tile([P, 2, 2, P], F32, tag="bank", name="xt_%d_%d_%d" % (s, g, half))
             banks[(s, g, half)] = bank
             for a in range(2):
                 for u in range(2):
-                    w0 = 256 * g + u
-                    nc.tensor.transpose(
-                        bank[:, a, u, :], words[:, 2 * half + a, w0 : 256 * g + 256 : 2], ident32[:]
-                    )
+                    nc.tensor.transpose(bank[:, a, u, :], words[:, 2 * half + a, u:256:2], ident32[:])
 
         def xc(s, g, half):
             if half == 0:
-                gxs[(s, g)] = gxp.tile([P, 512, 4], BF16, tag="gx", name="gx_%d_%d" % (s, g), align_bytes=64)
+                gxs[(s, g)] = grpp.tile([P, 512, 4], BF16, tag="grp", name="gx_%d_%d" % (s, g), align_bytes=64)
             gx32 = gxs[(s, g)][:].bitcast(F32)
             nc.scalar.copy(
                 out=gx32[:, 256 * half : 256 * half + 256, :].rearrange("p (a b) u -> p a b u", a=2),
@@ -230,10 +236,8 @@ def tile_slstmcell_pa_kernel(
         sb = {}
 
         def gate_act(g, m):
-            if g == GI:
-                dst = i_sb[m]
-            else:
-                dst = (fpool if g == GF else gatep).tile([P, 512], F32, tag="g%d" % g, name="gate_%d_%d" % (g, m))
+            pool, tag = (gatep, "z") if g == GZ else (fpool, "fi")
+            dst = pool.tile([P, 512], F32, tag=tag, name="gate_%d_%d" % (g, m))
             sb[(g, m)] = dst
             nc.scalar.activation(
                 out=dst[:],
@@ -283,7 +287,7 @@ def tile_slstmcell_pa_kernel(
             iz = gatep.tile([P, 512], F32, tag="iz", name="iz%d" % m)
             sb[("iz", m)] = iz
             eng = nc.gpsimd if m in GPSIMD_IZ else nc.vector
-            eng.tensor_tensor(out=iz[:], in0=i_sb[m][:], in1=sb[(GZ, m)][:], op=ALU.mult)
+            eng.tensor_tensor(out=iz[:], in0=sb[(GI, m)][:], in1=sb[(GZ, m)][:], op=ALU.mult)
 
         def v_c(m):
             nc.vector.tensor_tensor(
@@ -309,45 +313,9 @@ def tile_slstmcell_pa_kernel(
                 for half in range(2):
                     xt(0, g, half)
                     xc(0, g, half)
-        issue_next_load()
-        q_unit(GF, 1)
-        xq(0, 0)
-        rg_unit(GF, 2, V_COLS_F)
-        xq(0, 1)
-        passes(GF, 0, LO)
-        rg_unit(GF, 3, V_COLS_F)
-        issue_next_load()
-        q_unit(GF, 2)
-        for g in range(2):
-            for half in range(2):
-                xt(1, g, half)
-                xc(1, g, half)
-        issue_next_load()
-        passes(GF, 1, LO)
-        q_unit(GF, 3)
-        xq(1, 0)
-        rg_unit(GF, 4, V_COLS_F)
-        xq(1, 1)
-        bias_ps = trp.tile([P, P], BF16, tag="bank")
-        nc.tensor.transpose(bias_ps[:], bias_rows[:], ident16[:])
-        nc.vector.tensor_copy(out=bias_sb[:], in_=bias_ps[:, 0:24])
-        passes(GF, 0, HI)
-        passes(GF, 1, HI)
-        rg_unit(GF, 5, V_COLS_F)
-        issue_next_load()
-        q_unit(GF, 4)
-        passes(GF, 2, LO)
-        rg_unit(GF, 6, V_COLS_F)
-        q_unit(GF, 5)
-        passes(GF, 2, HI)
-        rg_unit(GF, 7, V_COLS_F)
-        issue_next_load()
-        q_unit(GF, 6)
-        passes(GF, 3, LO)
-
         EARLY, LATE = (0, 1, 2, 3, 4, 5), (6, 7)
-        for s in range(8):
-            rg_unit(GI, s, V_COLS_I)
+        def second_gate_step(s):
+            rg_unit(GI, s, V_COLS_I[s])
             if s % 2 == 1:
                 issue_next_load()
             if s == 0:
@@ -356,18 +324,57 @@ def tile_slstmcell_pa_kernel(
             else:
                 q_unit(GI, s - 1)
                 passes(GI, (s - 1) // 2, [m for m in (LO, HI)[(s - 1) % 2] if m in EARLY])
-            if s < 4:
-                for m in (2 * s, 2 * s + 1):
-                    gate_act(GF, m)
-                    flip((GF, m))
-            if 0 < s < 5:
-                v_fc_fn(2 * s - 2)
-                v_fc_fn(2 * s - 1)
+            for m in F_ACTS.get(s, ()):
+                gate_act(GF, m)
+                flip((GF, m))
+            for m in F_PRODUCTS.get(s, ()):
+                v_fc_fn(m)
             if s == 5:
                 passes(GI, 0, LATE)
                 passes(GI, 1, LATE)
             if s == 6:
                 passes(GI, 2, LATE)
+
+        with tc.manual_schedule(engines={mybir.EngineType.Activation}):
+            issue_next_load()
+            q_unit(GF, 1)
+            xq(0, 0)
+            rg_unit(GF, 2, V_COLS_F)
+            xq(0, 1)
+            passes(GF, 0, LO)
+            rg_unit(GF, 3, V_COLS_F)
+            issue_next_load()
+            q_unit(GF, 2)
+            for g in range(2):
+                for half in range(2):
+                    xt(1, g, half)
+                    xc(1, g, half)
+            issue_next_load()
+            passes(GF, 1, LO)
+            q_unit(GF, 3)
+            xq(1, 0)
+            rg_unit(GF, 4, V_COLS_F)
+            xq(1, 1)
+            bias_ps = trp.tile([P, P], BF16, tag="bank")
+            nc.tensor.transpose(bias_ps[:], bias_rows[:], ident16[:])
+            nc.vector.tensor_copy(out=bias_sb[:], in_=bias_ps[:, 0:24])
+            passes(GF, 0, HI)
+            passes(GF, 1, HI)
+            rg_unit(GF, 5, V_COLS_F)
+            issue_next_load()
+            q_unit(GF, 4)
+            passes(GF, 2, LO)
+            rg_unit(GF, 6, V_COLS_F)
+            q_unit(GF, 5)
+            passes(GF, 2, HI)
+            rg_unit(GF, 7, V_COLS_F)
+            issue_next_load()
+            q_unit(GF, 6)
+            passes(GF, 3, LO)
+            for s in range(2):
+                second_gate_step(s)
+        for s in range(2, 8):
+            second_gate_step(s)
 
         for m in range(LOOK + 1):
             rg_ztile(m, Z_V_CHUNKS[m])

@@ -18,13 +18,12 @@ RAW_SLOTS = 6
 PINNED = False
 V_COLS_F = 288
 V_COLS_I = (384, 384, 160, 160, 160, 160, 160, 160)
-Z_V_CHUNKS = (2, 1, 2, 1, 2, 1, 2, 1)
+Z_V_CHUNKS = (2, 1, 2, 1, 1, 2, 2, 2)
 GPSIMD_IZ = (0, 1, 2, 3, 4, 5, 6)
 STORES = ((0, 1), (2, 3), (4, 5), (6,), (7,))
 F_BUFS = 8
 GRP_BUFS = 7
 FIRST_LOADS = 6
-LOOK = 2
 F_ACTS = {0: (0, 1), 1: (2, 3, 4, 5, 6, 7)}
 F_PRODUCTS = {1: (0, 1), 2: (2, 3), 3: (4, 5), 4: (6, 7)}
 GF, GI, GZ = 0, 1, 2
@@ -67,14 +66,14 @@ def tile_slstmcell_pa_kernel(
         planes = [keep.tile([P, 1024], U8, name="planes%d" % c, align_bytes=64) for c in range(12)]
         xcodes = [keep.tile([P, 512], U32, name="xcodes%d" % c, align_bytes=64) for c in range(4)]
         xplanes = [keep.tile([P, 512], U8, name="xplanes%d" % c, align_bytes=64) for c in range(4)]
-        cn_sb = keep.tile([P, 2, 4, 1024], BF16)
+        cn_sb = [keep.tile([P, 2, 4, 512], BF16, name="cn_sb%d" % half) for half in range(2)]
         cn_out = [keep.tile([P, 2, 4, P * len(grp)], F32, name="cn_out%d" % grp[0]) for grp in STORES]
 
         out_c = out_0.rearrange("(p a) h -> p a h", a=4)
         out_n = out_1.rearrange("(p a) h -> p a h", a=4)
 
         load_order = [("w", 0, 0), ("a", 0, 0), ("w", 0, 1), ("a", 1, 0), ("w", 0, 2), ("w", 0, 3)]
-        load_order += [("w", 1, 0), ("c", 0, 0), ("c", 1, 0), ("w", 1, 1), ("w", 1, 2), ("w", 1, 3)]
+        load_order += [("w", 1, 0), ("c", 0, 0), ("c", 1, 0), ("w", 1, 1), ("c", 0, 1), ("c", 1, 1), ("w", 1, 2), ("w", 1, 3)]
         load_order += [("w", 2, c) for c in range(4)]
         raw_tiles = {}
         state = {"load": 0}
@@ -87,7 +86,9 @@ def tile_slstmcell_pa_kernel(
             kind, g, c = load_order[k]
             if kind == "c":
                 src = (c_prev, n_prev)[g]
-                nc.sync.dma_start(out=cn_sb[:, g], in_=src.rearrange("(p a) h -> p a h", a=4))
+                nc.sync.dma_start(
+                    out=cn_sb[c][:, g], in_=src[:, 512 * c : 512 * c + 512].rearrange("(p a) h -> p a h", a=4)
+                )
                 issue_next_load()
                 return
             if k == 0:
@@ -273,7 +274,7 @@ def tile_slstmcell_pa_kernel(
             nc.vector.tensor_tensor(
                 out=part(m),
                 in0=fT[:].unsqueeze(1).to_broadcast([P, 2, 4, P]),
-                in1=cn_sb[:, :, :, P * m : P * m + P],
+                in1=cn_sb[m // 4][:, :, :, P * (m % 4) : P * (m % 4) + P],
                 op=ALU.mult,
             )
 
@@ -376,28 +377,34 @@ def tile_slstmcell_pa_kernel(
         for s in range(2, 8):
             second_gate_step(s)
 
-        for m in range(LOOK + 1):
-            rg_ztile(m, Z_V_CHUNKS[m])
-            if m == 0:
-                q_unit(GI, 7)
-                passes(GI, 3, HI)
-        for m in range(LOOK):
-            q_ztile(m)
-            mx(GZ, m)
-        gate_act(GI, 0)
-        flip((GI, 0))
-        for s in range(8):
-            if s + LOOK < 8:
-                q_ztile(s + LOOK)
-                mx(GZ, s + LOOK)
-            if s + LOOK + 1 < 8:
-                rg_ztile(s + LOOK + 1, Z_V_CHUNKS[s + LOOK + 1])
-            gate_act(GZ, s)
-            if s < 7:
-                gate_act(GI, s + 1)
-            v_iz(s)
-            flip(("iz", s))
-            if s < 7:
-                flip((GI, s + 1))
-            v_n(s)
-            v_c(s)
+        with tc.manual_schedule(engines={mybir.EngineType.Activation, mybir.EngineType.PE}):
+            rg_ztile(0, Z_V_CHUNKS[0])
+            q_unit(GI, 7)
+            passes(GI, 3, HI)
+            rg_ztile(1, Z_V_CHUNKS[1])
+            rg_ztile(2, Z_V_CHUNKS[2])
+            gate_act(GI, 0)
+            flip((GI, 0))
+            gate_act(GI, 1)
+            for m in range(2):
+                q_ztile(m)
+                mx(GZ, m)
+            for s in range(8):
+                if s + 3 < 8:
+                    rg_ztile(s + 3, Z_V_CHUNKS[s + 3])
+                if s + 2 < 8:
+                    q_ztile(s + 2)
+                    mx(GZ, s + 2)
+                gate_act(GZ, s)
+                if s + 2 < 8:
+                    gate_act(GI, s + 2)
+                v_iz(s)
+                if s > 0:
+                    flip(("iz", s - 1))
+                if s < 7:
+                    flip((GI, s + 1))
+                v_n(s)
+                if s > 0:
+                    v_c(s - 1)
+            flip(("iz", 7))
+            v_c(7)

@@ -115,11 +115,10 @@ def tile_slstmcell_pa_kernel(
             else:
                 src = x if g == 0 else h_prev
                 for half in range(2):
-                    k0 = 512 * half
-                    piece = halfp.tile([P, 4, 512], BF16, tag="half", name="half_%d_%d" % (g, half))
+                    piece = halfp.tile([P, 2, 1024], BF16, tag="half", name="half_%d_%d" % (g, half))
                     raw_tiles[("half", g, half)] = piece
                     nc.sync.dma_start(
-                        out=piece[:], in_=src[:, k0 : k0 + 512].rearrange("(p a) k -> p a k", a=4)
+                        out=piece[:], in_=src.rearrange("(p a) k -> p a k", a=4)[:, 2 * half : 2 * half + 2, :]
                     )
 
         for k in range(FIRST_LOADS):
@@ -190,12 +189,12 @@ def tile_slstmcell_pa_kernel(
         banks = {}
 
         def xt(s, g, half):
-            words = raw_tiles[("half", s, g)][:].bitcast(F32)
+            words = raw_tiles[("half", s, half)][:].bitcast(F32)
             bank = (trp, flexp)[half].tile([P, 2, 2, P], F32, tag="bank", name="xt_%d_%d_%d" % (s, g, half))
             banks[(s, g, half)] = bank
             for a in range(2):
                 for u in range(2):
-                    nc.tensor.transpose(bank[:, a, u, :], words[:, 2 * half + a, u:256:2], ident32[:])
+                    nc.tensor.transpose(bank[:, a, u, :], words[:, a, 256 * g + u : 256 * g + 256 : 2], ident32[:])
 
         def xc(s, g, half):
             if half == 0:

@@ -295,6 +295,48 @@ def tile_slstmcell_pa_kernel(
             )
             store_if_full(0, m)
 
+        last = {}
+
+        def last_mx():
+            for half in range(2):
+                acc = accp.tile([P, 512], F32, tag="bank", name="acc_last%d" % half)
+                last[("acc", half)] = acc
+                cols = slice(256 * half, 256 * half + 256)
+                for c in range(4):
+                    lhsT, lhsT_scale = stationary(GZ, 7, c)
+                    nc.tensor.matmul_mx(
+                        out=acc[:, 0:256],
+                        lhsT=lhsT,
+                        lhsT_scale=lhsT_scale,
+                        rhs=xcodes[c][:, cols].bitcast(FP8X4),
+                        rhs_scale=xplanes[c][:, cols],
+                        start=(c == 0),
+                        stop=(c == 3),
+                    )
+
+        def last_act_iz():
+            z = gatep.tile([P, 512], F32, tag="z", name="z_last")
+            iz = gatep.tile([P, 512], F32, tag="iz", name="iz_last")
+            last["iz"] = iz
+            for half in range(2):
+                cols = slice(256 * half, 256 * half + 256)
+                nc.scalar.activation(
+                    out=z[:, cols], in_=last[("acc", half)][:, 0:256], func=ACT.Tanh, bias=bias_sb[:, 23:24], scale=1.0
+                )
+                nc.vector.tensor_tensor(out=iz[:, cols], in0=sb[(GI, 7)][:, cols], in1=z[:, cols], op=ALU.mult)
+
+        def last_flip(half):
+            bank = accp.tile([P, 4, P], F32, tag="bank", name="T_last%d" % half)
+            last[("T", half)] = bank
+            for a in range(2):
+                b0 = 256 * half + P * a
+                nc.tensor.transpose(bank[:, a, :], last["iz"][:, b0 : b0 + P], ident32[:])
+
+        def last_c(half):
+            dst = part(7)[:, 0, 2 * half : 2 * half + 2]
+            nc.vector.tensor_tensor(out=dst, in0=last[("T", half)][:, 0:2, :], in1=dst, op=ALU.add)
+            nc.sync.dma_start(out=out_c[:, 2 * half : 2 * half + 2, 7 * P : 8 * P], in_=dst)
+
         def passes(g, c, tiles):
             for m in tiles:
                 mx_pass(g, m, c)
@@ -393,11 +435,18 @@ def tile_slstmcell_pa_kernel(
                     rg_ztile(s + 3, Z_V_CHUNKS[s + 3])
                 if s + 2 < 8:
                     q_ztile(s + 2)
-                    mx(GZ, s + 2)
-                gate_act(GZ, s)
+                    if s + 2 < 7:
+                        mx(GZ, s + 2)
+                    else:
+                        last_mx()
+                if s < 7:
+                    gate_act(GZ, s)
                 if s + 2 < 8:
                     gate_act(GI, s + 2)
-                v_iz(s)
+                if s < 7:
+                    v_iz(s)
+                else:
+                    last_act_iz()
                 if s > 0:
                     flip(("iz", s - 1))
                 if s < 7:
@@ -405,5 +454,6 @@ def tile_slstmcell_pa_kernel(
                 v_n(s)
                 if s > 0:
                     v_c(s - 1)
-            flip(("iz", 7))
-            v_c(7)
+            for half in range(2):
+                last_flip(half)
+                last_c(half)

@@ -21,6 +21,8 @@ V_COLS_I = (384, 384, 160, 160, 160, 160, 160, 160)
 Z_V_CHUNKS = (2, 1, 2, 1, 1, 2, 2, 2)
 GPSIMD_IZ = (0, 1, 2, 3, 4, 5, 6)
 STORES = ((0, 1), (2, 3), (4, 5), (6,), (7,))
+NEW = (7,)
+V_EVACS = ()
 F_BUFS = 8
 GRP_BUFS = 7
 FIRST_LOADS = 6
@@ -249,13 +251,6 @@ def tile_slstmcell_pa_kernel(
 
         flipped = {}
 
-        def flip(key, pool=None):
-            bank = (pool or trp).tile([P, 4, P], F32, tag="bank", name="T_%s_%d" % key)
-            flipped[key] = bank
-            src = sb[key]
-            for a in range(4):
-                nc.tensor.transpose(bank[:, a, :], src[:, P * a : P * a + P], ident32[:])
-
         def part(m):
             for j, grp in enumerate(STORES):
                 if m in grp:
@@ -268,32 +263,67 @@ def tile_slstmcell_pa_kernel(
                     dram = (out_c, out_n)[which]
                     nc.sync.dma_start(out=dram[:, :, P * grp[0] : P * grp[-1] + P], in_=cn_out[j][:, which])
 
+        def flip(m):
+            if m in NEW:
+                bank = accp.tile([P, 2, 4, P], BF16, tag="bank", name="T_cn_%d" % m)
+                for g in range(2):
+                    for a in range(4):
+                        src = cn_sb[m // 4][:, g, a, P * (m % 4) : P * (m % 4) + P]
+                        nc.tensor.transpose(bank[:, g, a, :], src, ident16[:])
+            else:
+                bank = accp.tile([P, 4, P], F32, tag="bank", name="T_f_%d" % m)
+                for a in range(4):
+                    nc.tensor.transpose(bank[:, a, :], sb[(GF, m)][:, P * a : P * a + P], ident32[:])
+            flipped[m] = bank
+
         def v_fc_fn(m):
-            fT = flipped[(GF, m)]
+            if m in NEW:
+                in0 = sb[(GF, m)][:].rearrange("p (a b) -> p a b", a=4)
+                in1 = flipped[m][:]
+            else:
+                in0 = flipped[m][:]
+                in1 = cn_sb[m // 4][:, :, :, P * (m % 4) : P * (m % 4) + P]
             nc.vector.tensor_tensor(
-                out=part(m),
-                in0=fT[:].unsqueeze(1).to_broadcast([P, 2, 4, P]),
-                in1=cn_sb[m // 4][:, :, :, P * (m % 4) : P * (m % 4) + P],
-                op=ALU.mult,
+                out=part(m), in0=in0.unsqueeze(1).to_broadcast([P, 2, 4, P]), in1=in1, op=ALU.mult
             )
 
-        def v_n(m):
-            nc.vector.tensor_tensor(
-                out=part(m)[:, 1], in0=flipped[(GI, m)][:], in1=part(m)[:, 1], op=ALU.add
-            )
-            store_if_full(1, m)
+        def sum_flip(which, m):
+            bank = accp.tile([P, 4, P], F32, tag="bank", name="T_%s_%d" % ("cn"[which], m))
+            flipped[(which, m)] = bank
+            second = sb[(("iz", m), (GI, m))[which]]
+            for a in range(4):
+                cols = slice(P * a, P * a + P)
+                if m in NEW:
+                    nc.tensor.matmul(
+                        bank[:, a, :],
+                        lhsT=part(m)[:, which, a, :],
+                        rhs=ident32[:],
+                        is_transpose=True,
+                        start=True,
+                        stop=False,
+                    )
+                    nc.tensor.matmul(
+                        bank[:, a, :], lhsT=second[:, cols], rhs=ident32[:], is_transpose=True, start=False, stop=True
+                    )
+                else:
+                    nc.tensor.transpose(bank[:, a, :], second[:, cols], ident32[:])
+
+        def evacuate(which, m):
+            dst = part(m)[:, which]
+            bank = flipped[(which, m)]
+            if m not in NEW:
+                nc.vector.tensor_tensor(out=dst, in0=bank[:], in1=dst, op=ALU.add)
+            elif (which, m) in V_EVACS:
+                nc.vector.tensor_copy(out=dst, in_=bank[:])
+            else:
+                nc.scalar.copy(out=dst, in_=bank[:])
+            store_if_full(which, m)
 
         def v_iz(m):
             iz = gatep.tile([P, 512], F32, tag="iz", name="iz%d" % m)
             sb[("iz", m)] = iz
             eng = nc.gpsimd if m in GPSIMD_IZ else nc.vector
             eng.tensor_tensor(out=iz[:], in0=sb[(GI, m)][:], in1=sb[(GZ, m)][:], op=ALU.mult)
-
-        def v_c(m):
-            nc.vector.tensor_tensor(
-                out=part(m)[:, 0], in0=flipped[("iz", m)][:], in1=part(m)[:, 0], op=ALU.add
-            )
-            store_if_full(0, m)
 
         last = {}
 
@@ -330,11 +360,21 @@ def tile_slstmcell_pa_kernel(
             last[("T", half)] = bank
             for a in range(2):
                 b0 = 256 * half + P * a
-                nc.tensor.transpose(bank[:, a, :], last["iz"][:, b0 : b0 + P], ident32[:])
+                nc.tensor.matmul(
+                    bank[:, a, :],
+                    lhsT=part(7)[:, 0, 2 * half + a, :],
+                    rhs=ident32[:],
+                    is_transpose=True,
+                    start=True,
+                    stop=False,
+                )
+                nc.tensor.matmul(
+                    bank[:, a, :], lhsT=last["iz"][:, b0 : b0 + P], rhs=ident32[:], is_transpose=True, start=False, stop=True
+                )
 
         def last_c(half):
             dst = part(7)[:, 0, 2 * half : 2 * half + 2]
-            nc.vector.tensor_tensor(out=dst, in0=last[("T", half)][:, 0:2, :], in1=dst, op=ALU.add)
+            nc.scalar.copy(out=dst, in_=last[("T", half)][:, 0:2, :])
             nc.sync.dma_start(out=out_c[:, 2 * half : 2 * half + 2, 7 * P : 8 * P], in_=dst)
 
         def passes(g, c, tiles):
@@ -368,7 +408,7 @@ def tile_slstmcell_pa_kernel(
                 passes(GI, (s - 1) // 2, [m for m in (LO, HI)[(s - 1) % 2] if m in EARLY])
             for m in F_ACTS.get(s, ()):
                 gate_act(GF, m)
-                flip((GF, m))
+                flip(m)
             for m in F_PRODUCTS.get(s, ()):
                 v_fc_fn(m)
             if s == 5:
@@ -425,7 +465,7 @@ def tile_slstmcell_pa_kernel(
             rg_ztile(1, Z_V_CHUNKS[1])
             rg_ztile(2, Z_V_CHUNKS[2])
             gate_act(GI, 0)
-            flip((GI, 0))
+            sum_flip(1, 0)
             gate_act(GI, 1)
             for m in range(2):
                 q_ztile(m)
@@ -448,12 +488,12 @@ def tile_slstmcell_pa_kernel(
                 else:
                     last_act_iz()
                 if s > 0:
-                    flip(("iz", s - 1))
+                    sum_flip(0, s - 1)
                 if s < 7:
-                    flip((GI, s + 1))
-                v_n(s)
+                    sum_flip(1, s + 1)
+                evacuate(1, s)
                 if s > 0:
-                    v_c(s - 1)
+                    evacuate(0, s - 1)
             for half in range(2):
                 last_flip(half)
                 last_c(half)

from contextlib import ExitStack

import concourse.mybir as mybir
from concourse.masks import make_identity

FLOPS = 6 * 2 * 512 * 1024 * 1024

BF16 = mybir.dt.bfloat16
F32 = mybir.dt.float32
U32 = mybir.dt.uint32
U8 = mybir.dt.uint8
FP8X4 = mybir.dt.float8_e4m3fn_x4
ACT = mybir.ActivationFunctionType
ALU = mybir.AluOpType

P = 128
RAW_SLOTS = 6
PINNED = False
V_COLS_F = 288
V_COLS_I = (384, 384, 160, 160, 160, 160, 160, 160)
Z_V_CHUNKS = (2, 1, 2, 1, 1, 2, 2, 2)
GPSIMD_IZ = (0, 1, 2, 3, 4, 5, 6)
STORES = ((0, 1), (2, 3), (4, 5), (6,), (7,))
NEW = (7,)
V_EVACS = ()
F_BUFS = 8
GRP_BUFS = 7
FIRST_LOADS = 6
F_ACTS = {0: (0, 1), 1: (2, 3, 4, 5, 6, 7)}
F_PRODUCTS = {1: (0, 1), 2: (2, 3), 3: (4, 5), 4: (6, 7)}
GF, GI, GZ = 0, 1, 2
WARM_UP = 10


def tile_slstmcell_pa_kernel(
    tc, x, h_prev, c_prev, n_prev, W_i, b_i, U_i, W_f, b_f, U_f, W_z, b_z, U_z, out_0, out_1
):
    nc = tc.nc
    with ExitStack() as ctx:
        if PINNED:
            ctx.enter_context(tc.manual_schedule())
        const = ctx.enter_context(tc.tile_pool(name="const", bufs=1))
        keep = ctx.enter_context(tc.tile_pool(name="keep", bufs=1))
        rawp = ctx.enter_context(tc.tile_pool(name="rawp", bufs=RAW_SLOTS))
        halfp = ctx.enter_context(tc.tile_pool(name="halfp", bufs=4))
        grpp = ctx.enter_context(tc.tile_pool(name="grpp", bufs=GRP_BUFS))
        gatep = ctx.enter_context(tc.tile_pool(name="gatep", bufs=2))
        accp = ctx.enter_context(tc.psum_pool(name="psum", bufs=8))
        trp = accp
        flexp = accp
        fpool = ctx.enter_context(tc.tile_pool(name="fpool", bufs=F_BUFS))

        weights = ((W_f, U_f), (W_i, U_i), (W_z, U_z))
        biases = (b_f, b_i, b_z)

        bias_rows = const.tile([P, P], BF16)
        nc.vector.memset(bias_rows[:], 0.0)
        ident32 = const.tile([P, P], F32)
        make_identity(nc, ident32[:])
        ident16 = const.tile([P, P], BF16)
        make_identity(nc, ident16[:])
        bias_sb = const.tile([P, 24], F32)
        zeros = const.tile([P, 512], BF16)
        nc.vector.memset(zeros[:], 0.0)
        warm_act = const.tile([P, 1], F32)

        codes = [keep.tile([P, 1024], U32, name="codes%d" % c, align_bytes=64) for c in range(12)]
        planes = [keep.tile([P, 1024], U8, name="planes%d" % c, align_bytes=64) for c in range(12)]
        xcodes = [keep.tile([P, 512], U32, name="xcodes%d" % c, align_bytes=64) for c in range(4)]
        xplanes = [keep.tile([P, 512], U8, name="xplanes%d" % c, align_bytes=64) for c in range(4)]
        cn_sb = [keep.tile([P, 2, 4, 512], BF16, name="cn_sb%d" % half) for half in range(2)]
        cn_out = [keep.tile([P, 2, 4, P * len(grp)], F32, name="cn_out%d" % grp[0]) for grp in STORES]

        out_c = out_0.rearrange("(p a) h -> p a h", a=4)
        out_n = out_1.rearrange("(p a) h -> p a h", a=4)

        load_order = [("w", 0, 0), ("a", 0, 0), ("w", 0, 1), ("a", 1, 0), ("w", 0, 2), ("w", 0, 3)]
        load_order += [("w", 1, 0), ("c", 0, 0), ("c", 1, 0), ("w", 1, 1), ("c", 0, 1), ("c", 1, 1), ("w", 1, 2), ("w", 1, 3)]
        load_order += [("w", 2, c) for c in range(4)]
        raw_tiles = {}
        state = {"load": 0}

        def issue_next_load():
            k = state["load"]
            if k >= len(load_order):
                return
            state["load"] = k + 1
            kind, g, c = load_order[k]
            if kind == "c":
                src = (c_prev, n_prev)[g]
                nc.sync.dma_start(
                    out=cn_sb[c][:, g], in_=src[:, 512 * c : 512 * c + 512].rearrange("(p a) h -> p a h", a=4)
                )
                issue_next_load()
                return
            if k == 0:
                halves = rawp.tile([P, 2, 4, 512], BF16, tag="raw")
                raw_tiles["first"] = halves
                for b in range(2):
                    for u in range(2):
                        nc.sync.dma_start(
                            out=halves[:, b, 2 * u : 2 * u + 2, :],
                            in_=weights[0][0][0:512, 512 * b : 512 * b + 512].rearrange(
                                "(p e) n -> p e n", e=4
                            )[:, 2 * u : 2 * u + 2, :],
                        )
                return
            if kind == "w":
                raw = rawp.tile([P, 4, 1024], BF16, tag="raw", name="raw%d" % k)
                raw_tiles[load_order[k]] = raw
                w = weights[g][c // 2]
                r0 = 512 * (c % 2)
                nc.sync.dma_start(
                    out=raw[:],
                    in_=w[r0 : r0 + 512, :].rearrange("(p e) n -> p e n", e=4),
                )
            else:
                src = x if g == 0 else h_prev
                for half in range(2):
                    piece = halfp.tile([P, 2, 1024], BF16, tag="half", name="half_%d_%d" % (g, half))
                    raw_tiles[("half", g, half)] = piece
                    nc.sync.dma_start(
                        out=piece[:], in_=src.rearrange("(p a) k -> p a k", a=4)[:, 2 * half : 2 * half + 2, :]
                    )

        for k in range(FIRST_LOADS):
            issue_next_load()
            if k == 1:
                for g in range(3):
                    nc.sync.dma_start(
                        out=bias_rows[8 * g : 8 * g + 8, :],
                        in_=biases[g].rearrange("(m c) -> m c", c=P),
                    )

        def regroup(eng, dst, src):
            o = dst.rearrange("p (c i) t -> p c t i", i=4)
            s = src.rearrange("p t (c i) -> p c t i", i=4)
            if eng == "v":
                nc.vector.tensor_copy(out=o, in_=s)
            else:
                nc.scalar.copy(out=o, in_=s)

        grps = {}

        def rg_unit(g, u, vcols):
            c, c0 = u // 2, 512 * (u % 2)
            if g == 0 and c == 0:
                src = raw_tiles["first"][:, u]
            else:
                src = raw_tiles[("w", g, c)][:, :, c0 : c0 + 512]
            grp = grpp.tile([P, 512, 4], BF16, tag="grp", name="grp_%d_%d" % (g, u), align_bytes=64)
            grps[(g, u)] = grp
            regroup("v", grp[:, 0:vcols, :], src[:, :, 0:vcols])
            regroup("s", grp[:, vcols:512, :], src[:, :, vcols:512])

        def q_unit(g, u):
            c, c0 = u // 2, 512 * (u % 2)
            nc.vector.quantize_mx(
                out=codes[4 * g + c][:, c0 : c0 + 512].bitcast(FP8X4),
                scales=planes[4 * g + c][:, c0 : c0 + 512],
                in_=grps[(g, u)][:].rearrange("p w t -> p (w t)"),
            )

        def rg_ztile(m, v_chunks):
            grp = grpp.tile([P, 512, 4], BF16, tag="grp", name="grp_z_%d" % m, align_bytes=64)
            grps[(GZ, m)] = grp
            for c in range(4):
                raw = raw_tiles[("w", GZ, c)]
                regroup(
                    "v" if c >= 4 - v_chunks else "s",
                    grp[:, P * c : P * c + P, :],
                    raw[:, :, P * m : P * m + P],
                )

        def q_ztile(m):
            c0 = 512 * (m % 2)
            nc.vector.quantize_mx(
                out=codes[8 + m // 2][:, c0 : c0 + 512].bitcast(FP8X4),
                scales=planes[8 + m // 2][:, c0 : c0 + 512],
                in_=grps[(GZ, m)][:].rearrange("p w t -> p (w t)"),
            )

        def stationary(g, m, c):
            if g == GZ:
                t, c0 = 8 + m // 2, 512 * (m % 2) + P * c
            else:
                t, c0 = 4 * g + c, P * m
            return codes[t][:, c0 : c0 + P].bitcast(FP8X4), planes[t][:, c0 : c0 + P]

        gxs = {}
        banks = {}

        def xt(s, g, half):
            words = raw_tiles[("half", s, half)][:].bitcast(F32)
            bank = (trp, flexp)[half].tile([P, 2, 2, P], F32, tag="bank", name="xt_%d_%d_%d" % (s, g, half))
            banks[(s, g, half)] = bank
            for a in range(2):
                for u in range(2):
                    nc.tensor.transpose(bank[:, a, u, :], words[:, a, 256 * g + u : 256 * g + 256 : 2], ident32[:])

        def xc(s, g, half):
            if half == 0:
                gxs[(s, g)] = grpp.tile([P, 512, 4], BF16, tag="grp", name="gx_%d_%d" % (s, g), align_bytes=64)
            gx32 = gxs[(s, g)][:].bitcast(F32)
            nc.scalar.copy(
                out=gx32[:, 256 * half : 256 * half + 256, :].rearrange("p (a b) u -> p a b u", a=2),
                in_=banks[(s, g, half)][:].rearrange("p a u b -> p a b u"),
            )

        def xq(s, g):
            nc.vector.quantize_mx(
                out=xcodes[2 * s + g][:].bitcast(FP8X4),
                scales=xplanes[2 * s + g][:],
                in_=gxs[(s, g)][:].rearrange("p w t -> p (w t)"),
            )

        accs = {}

        def mx_pass(g, m, c, pool=None):
            if c == 0:
                pl = pool or accp
                accs[(g, m)] = pl.tile([P, 512], F32, tag="bank", name="acc_%d_%d" % (g, m))
            lhsT, lhsT_scale = stationary(g, m, c)
            nc.tensor.matmul_mx(
                out=accs[(g, m)][:],
                lhsT=lhsT,
                lhsT_scale=lhsT_scale,
                rhs=xcodes[c][:].bitcast(FP8X4),
                rhs_scale=xplanes[c][:],
                start=(c == 0),
                stop=(c == 3),
            )

        def mx(g, m, pool=None):
            for c in range(4):
                mx_pass(g, m, c, pool)

        sb = {}

        def gate_act(g, m):
            pool, tag = (gatep, "z") if g == GZ else (fpool, "fi")
            dst = pool.tile([P, 512], F32, tag=tag, name="gate_%d_%d" % (g, m))
            sb[(g, m)] = dst
            nc.scalar.activation(
                out=dst[:],
                in_=accs[(g, m)][:],
                func=(ACT.Tanh if g == GZ else ACT.Exp),
                bias=bias_sb[:, 8 * g + m : 8 * g + m + 1],
                scale=1.0,
            )

        flipped = {}

        def part(m):
            for j, grp in enumerate(STORES):
                if m in grp:
                    off = P * grp.index(m)
                    return cn_out[j][:, :, :, off : off + P]

        def store_if_full(which, m):
            for j, grp in enumerate(STORES):
                if m == grp[-1]:
                    dram = (out_c, out_n)[which]
                    nc.sync.dma_start(out=dram[:, :, P * grp[0] : P * grp[-1] + P], in_=cn_out[j][:, which])

        def flip(m):
            if m in NEW:
                bank = accp.tile([P, 2, 4, P], BF16, tag="bank", name="T_cn_%d" % m)
                for g in range(2):
                    for a in range(4):
                        src = cn_sb[m // 4][:, g, a, P * (m % 4) : P * (m % 4) + P]
                        nc.tensor.transpose(bank[:, g, a, :], src, ident16[:])
            else:
                bank = accp.tile([P, 4, P], F32, tag="bank", name="T_f_%d" % m)
                for a in range(4):
                    nc.tensor.transpose(bank[:, a, :], sb[(GF, m)][:, P * a : P * a + P], ident32[:])
            flipped[m] = bank

        def v_fc_fn(m):
            if m in NEW:
                in0 = sb[(GF, m)][:].rearrange("p (a b) -> p a b", a=4)
                in1 = flipped[m][:]
            else:
                in0 = flipped[m][:]
                in1 = cn_sb[m // 4][:, :, :, P * (m % 4) : P * (m % 4) + P]
            nc.vector.tensor_tensor(
                out=part(m), in0=in0.unsqueeze(1).to_broadcast([P, 2, 4, P]), in1=in1, op=ALU.mult
            )

        def sum_flip(which, m):
            bank = accp.tile([P, 4, P], F32, tag="bank", name="T_%s_%d" % ("cn"[which], m))
            flipped[(which, m)] = bank
            second = sb[(("iz", m), (GI, m))[which]]
            for a in range(4):
                cols = slice(P * a, P * a + P)
                if m in NEW:
                    nc.tensor.matmul(
                        bank[:, a, :],
                        lhsT=part(m)[:, which, a, :],
                        rhs=ident32[:],
                        is_transpose=True,
                        start=True,
                        stop=False,
                    )
                    nc.tensor.matmul(
                        bank[:, a, :], lhsT=second[:, cols], rhs=ident32[:], is_transpose=True, start=False, stop=True
                    )
                else:
                    nc.tensor.transpose(bank[:, a, :], second[:, cols], ident32[:])

        def evacuate(which, m):
            dst = part(m)[:, which]
            bank = flipped[(which, m)]
            if m not in NEW:
                nc.vector.tensor_tensor(out=dst, in0=bank[:], in1=dst, op=ALU.add)
            elif (which, m) in V_EVACS:
                nc.vector.tensor_copy(out=dst, in_=bank[:])
            else:
                nc.scalar.copy(out=dst, in_=bank[:])
            store_if_full(which, m)

        def v_iz(m):
            iz = gatep.tile([P, 512], F32, tag="iz", name="iz%d" % m)
            sb[("iz", m)] = iz
            eng = nc.gpsimd if m in GPSIMD_IZ else nc.vector
            eng.tensor_tensor(out=iz[:], in0=sb[(GI, m)][:], in1=sb[(GZ, m)][:], op=ALU.mult)

        last = {}

        def last_mx():
            for half in range(2):
                acc = accp.tile([P, 512], F32, tag="bank", name="acc_last%d" % half)
                last[("acc", half)] = acc
                cols = slice(256 * half, 256 * half + 256)
                for c in range(4):
                    lhsT, lhsT_scale = stationary(GZ, 7, c)
                    nc.tensor.matmul_mx(
                        out=acc[:, 0:256],
                        lhsT=lhsT,
                        lhsT_scale=lhsT_scale,
                        rhs=xcodes[c][:, cols].bitcast(FP8X4),
                        rhs_scale=xplanes[c][:, cols],
                        start=(c == 0),
                        stop=(c == 3),
                    )

        def last_act_iz():
            z = gatep.tile([P, 512], F32, tag="z", name="z_last")
            iz = gatep.tile([P, 512], F32, tag="iz", name="iz_last")
            last["iz"] = iz
            for half in range(2):
                cols = slice(256 * half, 256 * half + 256)
                nc.scalar.activation(
                    out=z[:, cols], in_=last[("acc", half)][:, 0:256], func=ACT.Tanh, bias=bias_sb[:, 23:24], scale=1.0
                )
                nc.vector.tensor_tensor(out=iz[:, cols], in0=sb[(GI, 7)][:, cols], in1=z[:, cols], op=ALU.mult)

        def last_flip(half):
            bank = accp.tile([P, 4, P], F32, tag="bank", name="T_last%d" % half)
            last[("T", half)] = bank
            for a in range(2):
                b0 = 256 * half + P * a
                nc.tensor.matmul(
                    bank[:, a, :],
                    lhsT=part(7)[:, 0, 2 * half + a, :],
                    rhs=ident32[:],
                    is_transpose=True,
                    start=True,
                    stop=False,
                )
                nc.tensor.matmul(
                    bank[:, a, :], lhsT=last["iz"][:, b0 : b0 + P], rhs=ident32[:], is_transpose=True, start=False, stop=True
                )

        def last_c(half):
            dst = part(7)[:, 0, 2 * half : 2 * half + 2]
            nc.scalar.copy(out=dst, in_=last[("T", half)][:, 0:2, :])
            nc.sync.dma_start(out=out_c[:, 2 * half : 2 * half + 2, 7 * P : 8 * P], in_=dst)

        def passes(g, c, tiles):
            for m in tiles:
                mx_pass(g, m, c)

        LO, HI = (0, 1, 2, 3), (4, 5, 6, 7)
        with tc.manual_schedule(engines={mybir.EngineType.PE, mybir.EngineType.Activation}):
            nc.scalar.activation(out=warm_act[:], in_=zeros[:, 0:1], func=ACT.Exp)
            warm_bank = accp.tile([P, 512], F32, tag="bank")
            for j in range(WARM_UP):
                nc.tensor.matmul(warm_bank[:], lhsT=zeros[:, 0:P], rhs=zeros[:], start=True, stop=True)
            rg_unit(GF, 0, V_COLS_F)
            rg_unit(GF, 1, V_COLS_F)
            issue_next_load()
            q_unit(GF, 0)
            for g in range(2):
                for half in range(2):
                    xt(0, g, half)
                    xc(0, g, half)
        EARLY, LATE = (0, 1, 2, 3, 4, 5), (6, 7)
        def second_gate_step(s):
            rg_unit(GI, s, V_COLS_I[s])
            if s % 2 == 1:
                issue_next_load()
            if s == 0:
                q_unit(GF, 7)
                passes(GF, 3, HI)
            else:
                q_unit(GI, s - 1)
                passes(GI, (s - 1) // 2, [m for m in (LO, HI)[(s - 1) % 2] if m in EARLY])
            for m in F_ACTS.get(s, ()):
                gate_act(GF, m)
                flip(m)
            for m in F_PRODUCTS.get(s, ()):
                v_fc_fn(m)
            if s == 5:
                passes(GI, 0, LATE)
                passes(GI, 1, LATE)
            if s == 6:
                passes(GI, 2, LATE)

        with tc.manual_schedule(engines={mybir.EngineType.Activation}):
            issue_next_load()
            q_unit(GF, 1)
            xq(0, 0)
            rg_unit(GF, 2, V_COLS_F)
            xq(0, 1)
            passes(GF, 0, LO)
            rg_unit(GF, 3, V_COLS_F)
            issue_next_load()
            q_unit(GF, 2)
            for g in range(2):
                for half in range(2):
                    xt(1, g, half)
                    xc(1, g, half)
            issue_next_load()
            passes(GF, 1, LO)
            q_unit(GF, 3)
            xq(1, 0)
            rg_unit(GF, 4, V_COLS_F)
            xq(1, 1)
            bias_ps = trp.tile([P, P], BF16, tag="bank")
            nc.tensor.transpose(bias_ps[:], bias_rows[:], ident16[:])
            nc.vector.tensor_copy(out=bias_sb[:], in_=bias_ps[:, 0:24])
            passes(GF, 0, HI)
            passes(GF, 1, HI)
            rg_unit(GF, 5, V_COLS_F)
            issue_next_load()
            q_unit(GF, 4)
            passes(GF, 2, LO)
            rg_unit(GF, 6, V_COLS_F)
            q_unit(GF, 5)
            passes(GF, 2, HI)
            rg_unit(GF, 7, V_COLS_F)
            issue_next_load()
            q_unit(GF, 6)
            passes(GF, 3, LO)
            for s in range(2):
                second_gate_step(s)
        for s in range(2, 8):
            second_gate_step(s)

        with tc.manual_schedule(engines={mybir.EngineType.Activation, mybir.EngineType.PE}):
            rg_ztile(0, Z_V_CHUNKS[0])
            q_unit(GI, 7)
            passes(GI, 3, HI)
            rg_ztile(1, Z_V_CHUNKS[1])
            rg_ztile(2, Z_V_CHUNKS[2])
            gate_act(GI, 0)
            sum_flip(1, 0)
            gate_act(GI, 1)
            for m in range(2):
                q_ztile(m)
                mx(GZ, m)
            for s in range(8):
                if s + 3 < 8:
                    rg_ztile(s + 3, Z_V_CHUNKS[s + 3])
                if s + 2 < 8:
                    q_ztile(s + 2)
                    if s + 2 < 7:
                        mx(GZ, s + 2)
                    else:
                        last_mx()
                if s < 7:
                    gate_act(GZ, s)
                if s + 2 < 8:
                    gate_act(GI, s + 2)
                if s < 7:
                    v_iz(s)
                else:
                    last_act_iz()
                if s > 0:
                    sum_flip(0, s - 1)
                if s < 7:
                    sum_flip(1, s + 1)
                evacuate(1, s)
                if s > 0:
                    evacuate(0, s - 1)
            for half in range(2):
                last_flip(half)
                last_c(half)
